import numpy as np
import ml_dtypes


def mxq(x, axis, fmt="e4m3"):
    dtype, down = {"e4m3": (ml_dtypes.float8_e4m3fn, 7), "e5m2": (ml_dtypes.float8_e5m2, 14)}[fmt]
    v = np.moveaxis(np.asarray(x, np.float32).astype(ml_dtypes.bfloat16).astype(np.float64), axis, -1)
    blocks = v.reshape(v.shape[:-1] + (-1, 32))
    amax = np.abs(blocks).max(-1, keepdims=True)
    byte = np.maximum(np.where(amax > 0, np.frexp(amax)[1] - 1 + 127, 0) - down, 1)
    scale = np.exp2(byte - 127.0)
    codes = (blocks / scale).astype(np.float32).astype(dtype).astype(np.float64)
    return np.moveaxis((codes * scale).reshape(v.shape), -1, axis)


WIDE = False


def mx_kscale(k):
    if not WIDE:
        return np.ones(k)
    levels = np.array([10, -10, 5, -5, 0])
    a = np.random.permutation(np.resize(levels, k // 512 * 4)).reshape(k // 512, 4)
    idx = np.arange(k)
    return np.exp2(a[idx // 512, idx % 128 // 32])


BF16 = ml_dtypes.bfloat16


def bf(x):
    return np.asarray(x, np.float32).astype(BF16)


def f64(x):
    return np.asarray(x).astype(np.float64)


E2M1 = np.array([0.0, 0.5, 1.0, 1.5, 2.0, 3.0, 4.0, 6.0, -0.0, -0.5, -1.0, -1.5, -2.0, -3.0, -4.0, -6.0])


def pack_weight(w, fmt):
    k, n = w.shape
    w = f64(bf(w)).reshape(k // 32, 32, n)
    amax = np.abs(w).max(1)
    if fmt == "e4m3":
        byte = np.frexp(amax)[1] - 1 + 127 - 7
    else:
        mant, ex = np.frexp(amax / 6.0)
        byte = np.where(mant > 0.5, ex, ex - 1) + 127
    byte = np.clip(np.where(amax > 0, byte, 1), 1, 254)
    scaled = (w * np.exp2(127.0 - byte)[:, None, :]).reshape(k, n).astype(np.float32)
    by_word = np.ascontiguousarray(scaled.reshape(k // 512, 128, 4, n).transpose(0, 1, 3, 2))
    if fmt == "e4m3":
        words = by_word.astype(ml_dtypes.float8_e4m3fn).view(np.uint8)
    else:
        c = by_word.astype(ml_dtypes.float4_e2m1fn).view(np.uint8) & 0xF
        words = c[..., 0::2] | (c[..., 1::2] << 4)
    return np.ascontiguousarray(words), np.ascontiguousarray(byte.astype(np.uint8).reshape(k // 512, 16, n))


def unpack_weight(words, scales, fmt):
    g, p, n, _ = words.shape
    if fmt == "e4m3":
        vals = np.ascontiguousarray(words).view(ml_dtypes.float8_e4m3fn).astype(np.float64)
    else:
        nib = np.empty((g, p, n, 4), np.uint8)
        nib[..., 0::2] = words & 0xF
        nib[..., 1::2] = words >> 4
        vals = E2M1[nib]
    vals = vals * np.repeat(np.exp2(scales.astype(np.float64) - 127.0), 8, axis=1)[..., None]
    return vals.transpose(0, 1, 3, 2).reshape(g * 512, n)


B, C_IN, H, W, C_OUT = 4, 512, 64, 64, 128
E = 1


def _box_sum(x):
    b, h, w, c = x.shape
    xp = np.pad(x, ((0, 0), (1, 1), (1, 1), (0, 0)))
    out = np.zeros_like(x)
    for i in range(3):
        for j in range(3):
            out = out + xp[:, i:i + h, j:j + w, :]
    return out


def setup_inputs():
    s = mx_kscale(C_IN)
    x = bf(np.random.standard_normal((B, C_IN, H, W)) * s[None, :, None, None])
    stack = np.random.standard_normal((E, C_IN, C_OUT)) * 3.0 / np.sqrt(C_IN) / s[None, :, None]
    words, scales = pack_weight(stack.reshape(-1, C_OUT), "e4m3")
    return {"x": x, "weight_words": words, "weight_scales": scales}


def reference(x, weight_words, weight_scales):
    x = f64(x)
    weight = unpack_weight(weight_words, weight_scales, "e4m3").reshape(E, C_IN, C_OUT)
    b, c, h, w = x.shape
    o = weight.shape[-1]
    x1 = np.transpose(x, (0, 2, 3, 1))
    xw = mxq(x1, 3, "e4m3") @ weight[0]
    deg = _box_sum(np.ones((1, h, w, 1)))
    dinv = 1.0 / np.sqrt(deg)
    y = dinv * _box_sum(dinv * xw)
    return np.transpose(y, (0, 3, 1, 2)).reshape(b, o, w, h)

@@ -1,0 +1,211 @@
+import math
+from contextlib import ExitStack
+
+import concourse.mybir as mybir
+
+F32 = mybir.dt.float32
+BF16 = mybir.dt.bfloat16
+I32 = mybir.dt.int32
+U32 = mybir.dt.uint32
+U8 = mybir.dt.uint8
+FP8X4 = mybir.dt.float8_e4m3fn_x4
+ADD = mybir.AluOpType.add
+COPY = mybir.ActivationFunctionType.Copy
+
+P = 128
+PACK = 4
+IMAGES, C_IN, H, W, C_OUT = 4, 512, 64, 64, 128
+FLOPS = 2 * IMAGES * H * W * C_IN * C_OUT
+
+SLAB_ROWS = 16
+SLAB_PIXELS = SLAB_ROWS * W
+SLABS_PER_IMAGE = H // SLAB_ROWS
+N_SLABS = IMAGES * SLABS_PER_IMAGE
+BANK_ROWS = 8
+BANK_PIXELS = BANK_ROWS * W
+PADDED_ROWS = H + 2
+LOADS_AHEAD = 4
+
+VECTOR_PIXELS = 416
+
+NINTH = 1.0 / 9.0
+RIM = math.sqrt(1.5)
+
+PAIRS = W // 2
+HALF_SLOT = PAIRS + 2
+SLOT = 2 * HALF_SLOT
+ODD_AT = 1
+EVEN_AT = ODD_AT + PAIRS
+MAX_UNIT_ROWS = 3 * BANK_ROWS
+N_SUMS_TILES = 3
+
+
+def unit_rows(slab_in_image):
+    first = 0 if slab_in_image == 0 else slab_in_image * SLAB_ROWS - BANK_ROWS
+    last = H if slab_in_image == SLABS_PER_IMAGE - 1 else (slab_in_image + 1) * SLAB_ROWS - BANK_ROWS
+    return first, last
+
+
+def tile_gcn_layer_t_e_kernel(tc, x, weight_words, weight_scales, out):
+    nc = tc.nc
+    with ExitStack() as ctx:
+        keep = ctx.enter_context(tc.tile_pool(name="keep", bufs=1))
+        raw_pool = ctx.enter_context(tc.tile_pool(name="raw", bufs=LOADS_AHEAD + 1))
+        grouped_pool = ctx.enter_context(tc.tile_pool(name="grouped", bufs=4))
+        pair_pool = ctx.enter_context(tc.tile_pool(name="pair", bufs=3))
+        result_pool = ctx.enter_context(tc.tile_pool(name="result", bufs=4))
+        bank_pool = ctx.enter_context(tc.psum_pool(name="bank", bufs=6))
+        rim_pool = ctx.enter_context(tc.psum_pool(name="rim", bufs=2))
+
+        w_codes = keep.tile([P, C_OUT * PACK], U8, align_bytes=64)
+        w_scales = keep.tile([P, C_OUT], U8, align_bytes=64)
+        x_codes = keep.tile([P, IMAGES, PADDED_ROWS * W], U32, align_bytes=64)
+        x_scales = keep.tile([P, IMAGES, PADDED_ROWS * W], U8, align_bytes=64)
+        sums_tiles = [keep.tile([P, MAX_UNIT_ROWS + 1, SLOT], F32, name="sums%d" % n) for n in range(N_SUMS_TILES)]
+
+        raw_tiles = {}
+        grouped_tiles = {}
+        banks_of = {}
+        rim_of = {}
+
+        def load(slab):
+            image, part = divmod(slab, SLABS_PER_IMAGE)
+            raw = raw_pool.tile([P, PACK, SLAB_PIXELS], BF16)
+            pixels = slice(part * SLAB_PIXELS, (part + 1) * SLAB_PIXELS)
+            nc.sync.dma_start(out=raw[:], in_=x[image].rearrange("(p t) h w -> p t (h w)", t=PACK)[:, :, pixels])
+            raw_tiles[slab] = raw
+
+        def regroup(slab):
+            raw = raw_tiles[slab]
+            grouped = grouped_pool.tile([P, SLAB_PIXELS, PACK], BF16, align_bytes=64)
+            nc.vector.tensor_copy(
+                out=grouped[:, 0:VECTOR_PIXELS, :].rearrange("p (c i) t -> p c t i", i=4),
+                in_=raw[:, :, 0:VECTOR_PIXELS].rearrange("p t (c i) -> p c t i", i=4),
+            )
+            nc.scalar.copy(
+                out=grouped[:, VECTOR_PIXELS:SLAB_PIXELS, :].rearrange("p (c i) t -> p c t i", i=4),
+                in_=raw[:, :, VECTOR_PIXELS:SLAB_PIXELS].rearrange("p t (c i) -> p c t i", i=4),
+            )
+            grouped_tiles[slab] = grouped
+
+        def quantise(slab):
+            image, part = divmod(slab, SLABS_PER_IMAGE)
+            grouped = grouped_tiles[slab]
+            first = (1 + part * SLAB_ROWS) * W
+            columns = slice(first, first + SLAB_PIXELS)
+            nc.vector.quantize_mx(
+                out=x_codes[:, image, columns].bitcast(FP8X4),
+                scales=x_scales[:, image, columns],
+                in_=grouped[:].rearrange("p w t -> p (w t)"),
+            )
+
+        def multiply_window(acc, image, padded_row, n_pixels, start, stop):
+            columns = slice(padded_row * W, padded_row * W + n_pixels)
+            nc.tensor.matmul_mx(
+                out=acc,
+                lhsT=w_codes[:].bitcast(FP8X4),
+                lhsT_scale=w_scales[:],
+                rhs=x_codes[:, image, columns].bitcast(FP8X4),
+                rhs_scale=x_scales[:, image, columns],
+                start=start,
+                stop=stop,
+            )
+
+        def multiply(slab):
+            image, part = divmod(slab, SLABS_PER_IMAGE)
+            first, last = unit_rows(part)
+            banks = []
+            for row in range(first, last, BANK_ROWS):
+                acc = bank_pool.tile([P, BANK_PIXELS], F32)
+                for shift in range(3):
+                    multiply_window(acc[:], image, row + shift, BANK_PIXELS, shift == 0, shift == 2)
+                banks.append(acc)
+            banks_of[slab] = banks
+            if first == 0 or last == H:
+                rim = rim_pool.tile([P, W], F32)
+                multiply_window(rim[:], image, 1 if first == 0 else H, W, True, True)
+                rim_of[slab] = rim
+
+        def sort_by_parity(dst_rows, src, factor):
+            by_parity = src.rearrange("p (i m e) -> p e i m", m=PAIRS, e=2)
+            for parity, at in ((1, ODD_AT), (0, EVEN_AT)):
+                nc.scalar.activation(out=dst_rows[:, :, at : at + PAIRS], in_=by_parity[:, parity], func=COPY, scale=factor)
+
+        def leave_psum(slab):
+            sums = sums_tiles[slab % N_SUMS_TILES]
+            rows = 0
+            for acc in banks_of[slab]:
+                sort_by_parity(sums[:, rows : rows + BANK_ROWS, :], acc[:], NINTH)
+                rows += BANK_ROWS
+            if slab in rim_of:
+                sort_by_parity(sums[:, rows : rows + 1, :], rim_of[slab][:], NINTH * (RIM - 1.0))
+                rows += 1
+            rim_columns = sums[:, 0:rows, EVEN_AT - 1 : EVEN_AT + 1]
+            nc.scalar.mul(out=rim_columns, in_=rim_columns, mul=RIM)
+
+        def finish(slab):
+            image, part = divmod(slab, SLABS_PER_IMAGE)
+            first, last = unit_rows(part)
+            rows = last - first
+            sums = sums_tiles[slab % N_SUMS_TILES]
+            filled = slice(ODD_AT, EVEN_AT + PAIRS)
+            if first == 0 or last == H:
+                near = slice(0, 2) if first == 0 else slice(rows - 2, rows)
+                nc.vector.tensor_tensor(
+                    out=sums[:, near, filled],
+                    in0=sums[:, near, filled],
+                    in1=sums[:, rows : rows + 1, filled].to_broadcast([P, 2, W]),
+                    op=ADD,
+                )
+            pair = pair_pool.tile([P, MAX_UNIT_ROWS, PAIRS], F32)
+            nc.vector.tensor_tensor(
+                out=pair[:, 0:rows, :],
+                in0=sums[:, 0:rows, EVEN_AT : EVEN_AT + PAIRS],
+                in1=sums[:, 0:rows, ODD_AT : ODD_AT + PAIRS],
+                op=ADD,
+            )
+            result = result_pool.tile([P, MAX_UNIT_ROWS, W], F32)
+            neighbours = sums[:, 0:rows, :].rearrange("p i (e q) -> p i e q", e=2)[:, :, :, 0:PAIRS]
+            nc.vector.tensor_tensor(
+                out=result[:, 0:rows, :].rearrange("p i (m e) -> p i m e", e=2),
+                in0=pair[:, 0:rows, :].unsqueeze(3).to_broadcast([P, rows, PAIRS, 2]),
+                in1=neighbours.rearrange("p i e m -> p i m e"),
+                op=ADD,
+            )
+            rim_columns = result[:, 0:rows, 0 : W : W - 1]
+            nc.vector.tensor_scalar_mul(out=rim_columns, in0=rim_columns, scalar1=RIM)
+            if first == 0 or last == H:
+                rim_row = result[:, 0:1, :] if first == 0 else result[:, rows - 1 : rows, :]
+                nc.vector.tensor_scalar_mul(out=rim_row, in0=rim_row, scalar1=RIM)
+            nc.sync.dma_start(
+                out=out[image].rearrange("o h w -> o (h w)")[:, first * W : last * W],
+                in_=result[:, 0:rows, :].rearrange("p i j -> p (i j)"),
+            )
+
+        load(0)
+        nc.sync.dma_start(out=w_codes[:].bitcast(I32), in_=weight_words[0].rearrange("p n t -> p (n t)").bitcast(I32))
+        nc.vector.memset(w_scales[:].bitcast(I32), 0)
+        for quadrant in range(4):
+            nc.sync.dma_start(
+                out=w_scales[32 * quadrant : 32 * quadrant + 4, :].bitcast(I32),
+                in_=weight_scales[0, 4 * quadrant : 4 * quadrant + 4, :].bitcast(I32),
+            )
+        for slab in range(1, LOADS_AHEAD):
+            load(slab)
+        top_and_bottom = slice(0, PADDED_ROWS, PADDED_ROWS - 1)
+        nc.vector.memset(x_codes[:].bitcast(I32).rearrange("p b (r w) -> p b r w", r=PADDED_ROWS)[:, :, top_and_bottom, :], 0)
+        nc.vector.memset(x_scales[:].bitcast(I32).rearrange("p b (r w) -> p b r w", r=PADDED_ROWS)[:, :, top_and_bottom, :], 0)
+        for sums in sums_tiles:
+            nc.vector.memset(sums[:], 0.0)
+
+        for step in range(N_SLABS + 2):
+            if step + LOADS_AHEAD < N_SLABS:
+                load(step + LOADS_AHEAD)
+            if step < N_SLABS:
+                regroup(step)
+            if 1 <= step <= N_SLABS:
+                quantise(step - 1)
+                multiply(step - 1)
+                leave_psum(step - 1)
+            if step >= 2:
+                finish(step - 2)

@@ -27,6 +27,7 @@ PADDED_ROWS = H + 2
 LOADS_AHEAD = 4
 
 VECTOR_PIXELS = 416
+SCALAR_HALF = (SLAB_PIXELS - VECTOR_PIXELS) // 2
 
 NINTH = 1.0 / 9.0
 RIM = math.sqrt(1.5)
@@ -37,7 +38,7 @@ SLOT = 2 * HALF_SLOT
 ODD_AT = 1
 EVEN_AT = ODD_AT + PAIRS
 MAX_UNIT_ROWS = 3 * BANK_ROWS
-N_SUMS_TILES = 3
+N_SUMS_TILES = 4
 
 
 def unit_rows(slab_in_image):
@@ -67,6 +68,8 @@ def tile_gcn_layer_t_e_kernel(tc, x, weight_words, weight_scales, out):
         grouped_tiles = {}
         banks_of = {}
         rim_of = {}
+        pair_tiles = {}
+        result_tiles = {}
 
         def load(slab):
             image, part = divmod(slab, SLABS_PER_IMAGE)
@@ -75,18 +78,11 @@ def tile_gcn_layer_t_e_kernel(tc, x, weight_words, weight_scales, out):
             nc.sync.dma_start(out=raw[:], in_=x[image].rearrange("(p t) h w -> p t (h w)", t=PACK)[:, :, pixels])
             raw_tiles[slab] = raw
 
-        def regroup(slab):
-            raw = raw_tiles[slab]
-            grouped = grouped_pool.tile([P, SLAB_PIXELS, PACK], BF16, align_bytes=64)
-            nc.vector.tensor_copy(
-                out=grouped[:, 0:VECTOR_PIXELS, :].rearrange("p (c i) t -> p c t i", i=4),
-                in_=raw[:, :, 0:VECTOR_PIXELS].rearrange("p t (c i) -> p c t i", i=4),
+        def regroup(copy, slab, first, last):
+            copy(
+                out=grouped_tiles[slab][:, first:last, :].rearrange("p (c i) t -> p c t i", i=4),
+                in_=raw_tiles[slab][:, :, first:last].rearrange("p t (c i) -> p c t i", i=4),
             )
-            nc.scalar.copy(
-                out=grouped[:, VECTOR_PIXELS:SLAB_PIXELS, :].rearrange("p (c i) t -> p c t i", i=4),
-                in_=raw[:, :, VECTOR_PIXELS:SLAB_PIXELS].rearrange("p t (c i) -> p c t i", i=4),
-            )
-            grouped_tiles[slab] = grouped
 
         def quantise(slab):
             image, part = divmod(slab, SLABS_PER_IMAGE)
@@ -131,32 +127,42 @@ def tile_gcn_layer_t_e_kernel(tc, x, weight_words, weight_scales, out):
             for parity, at in ((1, ODD_AT), (0, EVEN_AT)):
                 nc.scalar.activation(out=dst_rows[:, :, at : at + PAIRS], in_=by_parity[:, parity], func=COPY, scale=factor)
 
+        def has_rim_row(slab):
+            return slab % SLABS_PER_IMAGE in (0, SLABS_PER_IMAGE - 1)
+
+        def n_rows(slab):
+            first, last = unit_rows(slab % SLABS_PER_IMAGE)
+            return last - first
+
         def leave_psum(slab):
             sums = sums_tiles[slab % N_SUMS_TILES]
             rows = 0
             for acc in banks_of[slab]:
                 sort_by_parity(sums[:, rows : rows + BANK_ROWS, :], acc[:], NINTH)
                 rows += BANK_ROWS
-            if slab in rim_of:
+            if has_rim_row(slab):
                 sort_by_parity(sums[:, rows : rows + 1, :], rim_of[slab][:], NINTH * (RIM - 1.0))
-                rows += 1
-            rim_columns = sums[:, 0:rows, EVEN_AT - 1 : EVEN_AT + 1]
+
+        def weigh_rim_columns(slab):
+            rows = n_rows(slab) + (1 if has_rim_row(slab) else 0)
+            rim_columns = sums_tiles[slab % N_SUMS_TILES][:, 0:rows, EVEN_AT - 1 : EVEN_AT + 1]
             nc.scalar.mul(out=rim_columns, in_=rim_columns, mul=RIM)
 
-        def finish(slab):
-            image, part = divmod(slab, SLABS_PER_IMAGE)
-            first, last = unit_rows(part)
-            rows = last - first
+        def add_rim_row(slab):
+            rows = n_rows(slab)
             sums = sums_tiles[slab % N_SUMS_TILES]
+            near = slice(0, 2) if slab % SLABS_PER_IMAGE == 0 else slice(rows - 2, rows)
             filled = slice(ODD_AT, EVEN_AT + PAIRS)
-            if first == 0 or last == H:
-                near = slice(0, 2) if first == 0 else slice(rows - 2, rows)
-                nc.vector.tensor_tensor(
-                    out=sums[:, near, filled],
-                    in0=sums[:, near, filled],
-                    in1=sums[:, rows : rows + 1, filled].to_broadcast([P, 2, W]),
-                    op=ADD,
-                )
+            nc.vector.tensor_tensor(
+                out=sums[:, near, filled],
+                in0=sums[:, near, filled],
+                in1=sums[:, rows : rows + 1, filled].to_broadcast([P, 2, W]),
+                op=ADD,
+            )
+
+        def add_pairs(slab):
+            rows = n_rows(slab)
+            sums = sums_tiles[slab % N_SUMS_TILES]
             pair = pair_pool.tile([P, MAX_UNIT_ROWS, PAIRS], F32)
             nc.vector.tensor_tensor(
                 out=pair[:, 0:rows, :],
@@ -164,27 +170,52 @@ def tile_gcn_layer_t_e_kernel(tc, x, weight_words, weight_scales, out):
                 in1=sums[:, 0:rows, ODD_AT : ODD_AT + PAIRS],
                 op=ADD,
             )
+            pair_tiles[slab] = pair
+
+        def add_neighbours(slab):
+            rows = n_rows(slab)
+            sums = sums_tiles[slab % N_SUMS_TILES]
             result = result_pool.tile([P, MAX_UNIT_ROWS, W], F32)
             neighbours = sums[:, 0:rows, :].rearrange("p i (e q) -> p i e q", e=2)[:, :, :, 0:PAIRS]
             nc.vector.tensor_tensor(
                 out=result[:, 0:rows, :].rearrange("p i (m e) -> p i m e", e=2),
-                in0=pair[:, 0:rows, :].unsqueeze(3).to_broadcast([P, rows, PAIRS, 2]),
+                in0=pair_tiles[slab][:, 0:rows, :].unsqueeze(3).to_broadcast([P, rows, PAIRS, 2]),
                 in1=neighbours.rearrange("p i e m -> p i m e"),
                 op=ADD,
             )
-            rim_columns = result[:, 0:rows, 0 : W : W - 1]
+            result_tiles[slab] = result
+
+        def scale_rim_row(slab):
+            row = 0 if slab % SLABS_PER_IMAGE == 0 else n_rows(slab) - 1
+            rim_row = result_tiles[slab][:, row : row + 1, :]
+            nc.vector.tensor_scalar_mul(out=rim_row, in0=rim_row, scalar1=RIM)
+
+        def scale_rim_columns(slab):
+            rim_columns = result_tiles[slab][:, 0 : n_rows(slab), 0 : W : W - 1]
             nc.vector.tensor_scalar_mul(out=rim_columns, in0=rim_columns, scalar1=RIM)
-            if first == 0 or last == H:
-                rim_row = result[:, 0:1, :] if first == 0 else result[:, rows - 1 : rows, :]
-                nc.vector.tensor_scalar_mul(out=rim_row, in0=rim_row, scalar1=RIM)
+
+        def store(slab):
+            image, part = divmod(slab, SLABS_PER_IMAGE)
+            first, last = unit_rows(part)
             nc.sync.dma_start(
                 out=out[image].rearrange("o h w -> o (h w)")[:, first * W : last * W],
-                in_=result[:, 0:rows, :].rearrange("p i j -> p (i j)"),
+                in_=result_tiles[slab][:, 0 : last - first, :].rearrange("p i j -> p (i j)"),
             )
+
+        def live(slab):
+            return 0 <= slab < N_SLABS
+
+        ctx.enter_context(tc.manual_schedule())
+
+        nc.vector.memset(w_scales[:].bitcast(I32), 0)
+        top_and_bottom = slice(0, PADDED_ROWS, PADDED_ROWS - 1)
+        nc.vector.memset(x_codes[:].bitcast(I32).rearrange("p b (r w) -> p b r w", r=PADDED_ROWS)[:, :, top_and_bottom, :], 0)
+        nc.vector.memset(x_scales[:].bitcast(I32).rearrange("p b (r w) -> p b r w", r=PADDED_ROWS)[:, :, top_and_bottom, :], 0)
+        for sums in sums_tiles:
+            nc.vector.memset(sums[:], 0.0)
 
         load(0)
         nc.sync.dma_start(out=w_codes[:].bitcast(I32), in_=weight_words[0].rearrange("p n t -> p (n t)").bitcast(I32))
-        nc.vector.memset(w_scales[:].bitcast(I32), 0)
         for quadrant in range(4):
             nc.sync.dma_start(
                 out=w_scales[32 * quadrant : 32 * quadrant + 4, :].bitcast(I32),
@@ -192,20 +223,31 @@ def tile_gcn_layer_t_e_kernel(tc, x, weight_words, weight_scales, out):
             )
         for slab in range(1, LOADS_AHEAD):
             load(slab)
-        top_and_bottom = slice(0, PADDED_ROWS, PADDED_ROWS - 1)
-        nc.vector.memset(x_codes[:].bitcast(I32).rearrange("p b (r w) -> p b r w", r=PADDED_ROWS)[:, :, top_and_bottom, :], 0)
-        nc.vector.memset(x_scales[:].bitcast(I32).rearrange("p b (r w) -> p b r w", r=PADDED_ROWS)[:, :, top_and_bottom, :], 0)
-        for sums in sums_tiles:
-            nc.vector.memset(sums[:], 0.0)
 
-        for step in range(N_SLABS + 2):
-            if step + LOADS_AHEAD < N_SLABS:
+        for step in range(N_SLABS + 4):
+            if live(step + LOADS_AHEAD):
                 load(step + LOADS_AHEAD)
-            if step < N_SLABS:
-                regroup(step)
-            if 1 <= step <= N_SLABS:
+            if live(step - 1):
                 quantise(step - 1)
                 multiply(step - 1)
+            if live(step - 4) and has_rim_row(step - 4):
+                scale_rim_row(step - 4)
+            if live(step):
+                grouped_tiles[step] = grouped_pool.tile([P, SLAB_PIXELS, PACK], BF16, align_bytes=64, name="grouped")
+                regroup(nc.scalar.copy, step, VECTOR_PIXELS, VECTOR_PIXELS + SCALAR_HALF)
+            if live(step - 2):
+                weigh_rim_columns(step - 2)
+            if live(step):
+                regroup(nc.scalar.copy, step, VECTOR_PIXELS + SCALAR_HALF, SLAB_PIXELS)
+                regroup(nc.vector.tensor_copy, step, 0, VECTOR_PIXELS)
+            if live(step - 1):
                 leave_psum(step - 1)
-            if step >= 2:
-                finish(step - 2)
+            if live(step - 2) and has_rim_row(step - 2):
+                add_rim_row(step - 2)
+            if live(step - 3):
+                add_neighbours(step - 3)
+            if live(step - 2):
+                add_pairs(step - 2)
+            if live(step - 4):
+                scale_rim_columns(step - 4)
+                store(step - 4)

@@ -26,7 +26,7 @@ BANK_PIXELS = BANK_ROWS * W
 PADDED_ROWS = H + 2
 LOADS_AHEAD = 4
 
-VECTOR_PIXELS = 416
+VECTOR_PIXELS = 480
 SCALAR_HALF = (SLAB_PIXELS - VECTOR_PIXELS) // 2
 
 NINTH = 1.0 / 9.0
@@ -38,7 +38,7 @@ SLOT = 2 * HALF_SLOT
 ODD_AT = 1
 EVEN_AT = ODD_AT + PAIRS
 MAX_UNIT_ROWS = 3 * BANK_ROWS
-N_SUMS_TILES = 4
+N_SUMS_TILES = 5
 
 
 def unit_rows(slab_in_image):
@@ -212,7 +212,8 @@ def tile_gcn_layer_t_e_kernel(tc, x, weight_words, weight_scales, out):
         nc.vector.memset(x_codes[:].bitcast(I32).rearrange("p b (r w) -> p b r w", r=PADDED_ROWS)[:, :, top_and_bottom, :], 0)
         nc.vector.memset(x_scales[:].bitcast(I32).rearrange("p b (r w) -> p b r w", r=PADDED_ROWS)[:, :, top_and_bottom, :], 0)
         for sums in sums_tiles:
-            nc.vector.memset(sums[:], 0.0)
+            nc.vector.memset(sums[:, :, 0 : ODD_AT + 1], 0.0)
+            nc.vector.memset(sums[:, :, EVEN_AT + PAIRS - 1 : EVEN_AT + PAIRS + 1], 0.0)
 
         load(0)
         nc.sync.dma_start(out=w_codes[:].bitcast(I32), in_=weight_words[0].rearrange("p n t -> p (n t)").bitcast(I32))
@@ -224,30 +225,30 @@ def tile_gcn_layer_t_e_kernel(tc, x, weight_words, weight_scales, out):
         for slab in range(1, LOADS_AHEAD):
             load(slab)
 
-        for step in range(N_SLABS + 4):
+        for step in range(N_SLABS + 7):
             if live(step + LOADS_AHEAD):
                 load(step + LOADS_AHEAD)
-            if live(step - 1):
-                quantise(step - 1)
-                multiply(step - 1)
-            if live(step - 4) and has_rim_row(step - 4):
-                scale_rim_row(step - 4)
+            if live(step - 2):
+                quantise(step - 2)
+                multiply(step - 2)
             if live(step):
                 grouped_tiles[step] = grouped_pool.tile([P, SLAB_PIXELS, PACK], BF16, align_bytes=64, name="grouped")
+                regroup(nc.vector.tensor_copy, step, 0, VECTOR_PIXELS)
                 regroup(nc.scalar.copy, step, VECTOR_PIXELS, VECTOR_PIXELS + SCALAR_HALF)
-            if live(step - 2):
-                weigh_rim_columns(step - 2)
+            if live(step - 4):
+                weigh_rim_columns(step - 4)
             if live(step):
                 regroup(nc.scalar.copy, step, VECTOR_PIXELS + SCALAR_HALF, SLAB_PIXELS)
-                regroup(nc.vector.tensor_copy, step, 0, VECTOR_PIXELS)
-            if live(step - 1):
-                leave_psum(step - 1)
-            if live(step - 2) and has_rim_row(step - 2):
-                add_rim_row(step - 2)
             if live(step - 3):
-                add_neighbours(step - 3)
-            if live(step - 2):
-                add_pairs(step - 2)
-            if live(step - 4):
-                scale_rim_columns(step - 4)
-                store(step - 4)
+                leave_psum(step - 3)
+            if live(step - 5) and has_rim_row(step - 5):
+                add_rim_row(step - 5)
+            if live(step - 6):
+                add_neighbours(step - 6)
+            if live(step - 5):
+                add_pairs(step - 5)
+            if live(step - 6):
+                if has_rim_row(step - 6):
+                    scale_rim_row(step - 6)
+                scale_rim_columns(step - 6)
+                store(step - 6)

@@ -205,7 +205,6 @@ def tile_gcn_layer_t_e_kernel(tc, x, weight_words, weight_scales, out):
         def live(slab):
             return 0 <= slab < N_SLABS
 
-        ctx.enter_context(tc.manual_schedule())
 
         nc.vector.memset(w_scales[:].bitcast(I32), 0)
         top_and_bottom = slice(0, PADDED_ROWS, PADDED_ROWS - 1)

@@ -26,7 +26,7 @@ BANK_PIXELS = BANK_ROWS * W
 PADDED_ROWS = H + 2
 LOADS_AHEAD = 4
 
-VECTOR_PIXELS = 480
+VECTOR_PIXELS = 544
 SCALAR_HALF = (SLAB_PIXELS - VECTOR_PIXELS) // 2
 
 NINTH = 1.0 / 9.0
@@ -188,11 +188,11 @@ def tile_gcn_layer_t_e_kernel(tc, x, weight_words, weight_scales, out):
         def scale_rim_row(slab):
             row = 0 if slab % SLABS_PER_IMAGE == 0 else n_rows(slab) - 1
             rim_row = result_tiles[slab][:, row : row + 1, :]
-            nc.vector.tensor_scalar_mul(out=rim_row, in0=rim_row, scalar1=RIM)
+            nc.scalar.mul(out=rim_row, in_=rim_row, mul=RIM)
 
         def scale_rim_columns(slab):
             rim_columns = result_tiles[slab][:, 0 : n_rows(slab), 0 : W : W - 1]
-            nc.vector.tensor_scalar_mul(out=rim_columns, in0=rim_columns, scalar1=RIM)
+            nc.scalar.mul(out=rim_columns, in_=rim_columns, mul=RIM)
 
         def store(slab):
             image, part = divmod(slab, SLABS_PER_IMAGE)

@@ -134,6 +134,11 @@ def tile_gcn_layer_t_e_kernel(tc, x, weight_words, weight_scales, out):
             first, last = unit_rows(slab % SLABS_PER_IMAGE)
             return last - first
 
+        def pieces(slab):
+            if slab == N_SLABS - 1:
+                return [(row, row + BANK_ROWS) for row in range(0, n_rows(slab), BANK_ROWS)]
+            return [(0, n_rows(slab))]
+
         def leave_psum(slab):
             sums = sums_tiles[slab % N_SUMS_TILES]
             rows = 0
@@ -144,9 +149,12 @@ def tile_gcn_layer_t_e_kernel(tc, x, weight_words, weight_scales, out):
                 sort_by_parity(sums[:, rows : rows + 1, :], rim_of[slab][:], NINTH * (RIM - 1.0))
 
         def weigh_rim_columns(slab):
-            rows = n_rows(slab) + (1 if has_rim_row(slab) else 0)
-            rim_columns = sums_tiles[slab % N_SUMS_TILES][:, 0:rows, EVEN_AT - 1 : EVEN_AT + 1]
-            nc.scalar.mul(out=rim_columns, in_=rim_columns, mul=RIM)
+            ranges = pieces(slab)
+            if has_rim_row(slab):
+                ranges = ranges[:-1] + [(ranges[-1][0], ranges[-1][1] + 1)]
+            for first, last in ranges:
+                rim_columns = sums_tiles[slab % N_SUMS_TILES][:, first:last, EVEN_AT - 1 : EVEN_AT + 1]
+                nc.scalar.mul(out=rim_columns, in_=rim_columns, mul=RIM)
 
         def add_rim_row(slab):
             rows = n_rows(slab)
@@ -161,28 +169,28 @@ def tile_gcn_layer_t_e_kernel(tc, x, weight_words, weight_scales, out):
             )
 
         def add_pairs(slab):
-            rows = n_rows(slab)
             sums = sums_tiles[slab % N_SUMS_TILES]
             pair = pair_pool.tile([P, MAX_UNIT_ROWS, PAIRS], F32)
-            nc.vector.tensor_tensor(
-                out=pair[:, 0:rows, :],
-                in0=sums[:, 0:rows, EVEN_AT : EVEN_AT + PAIRS],
-                in1=sums[:, 0:rows, ODD_AT : ODD_AT + PAIRS],
-                op=ADD,
-            )
+            for first, last in pieces(slab):
+                nc.vector.tensor_tensor(
+                    out=pair[:, first:last, :],
+                    in0=sums[:, first:last, EVEN_AT : EVEN_AT + PAIRS],
+                    in1=sums[:, first:last, ODD_AT : ODD_AT + PAIRS],
+                    op=ADD,
+                )
             pair_tiles[slab] = pair
 
         def add_neighbours(slab):
-            rows = n_rows(slab)
             sums = sums_tiles[slab % N_SUMS_TILES]
             result = result_pool.tile([P, MAX_UNIT_ROWS, W], F32)
-            neighbours = sums[:, 0:rows, :].rearrange("p i (e q) -> p i e q", e=2)[:, :, :, 0:PAIRS]
-            nc.vector.tensor_tensor(
-                out=result[:, 0:rows, :].rearrange("p i (m e) -> p i m e", e=2),
-                in0=pair_tiles[slab][:, 0:rows, :].unsqueeze(3).to_broadcast([P, rows, PAIRS, 2]),
-                in1=neighbours.rearrange("p i e m -> p i m e"),
-                op=ADD,
-            )
+            for first, last in pieces(slab):
+                neighbours = sums[:, first:last, :].rearrange("p i (e q) -> p i e q", e=2)[:, :, :, 0:PAIRS]
+                nc.vector.tensor_tensor(
+                    out=result[:, first:last, :].rearrange("p i (m e) -> p i m e", e=2),
+                    in0=pair_tiles[slab][:, first:last, :].unsqueeze(3).to_broadcast([P, last - first, PAIRS, 2]),
+                    in1=neighbours.rearrange("p i e m -> p i m e"),
+                    op=ADD,
+                )
             result_tiles[slab] = result
 
         def scale_rim_row(slab):
@@ -191,16 +199,18 @@ def tile_gcn_layer_t_e_kernel(tc, x, weight_words, weight_scales, out):
             nc.scalar.mul(out=rim_row, in_=rim_row, mul=RIM)
 
         def scale_rim_columns(slab):
-            rim_columns = result_tiles[slab][:, 0 : n_rows(slab), 0 : W : W - 1]
-            nc.scalar.mul(out=rim_columns, in_=rim_columns, mul=RIM)
+            for first, last in pieces(slab):
+                rim_columns = result_tiles[slab][:, first:last, 0 : W : W - 1]
+                nc.scalar.mul(out=rim_columns, in_=rim_columns, mul=RIM)
 
         def store(slab):
             image, part = divmod(slab, SLABS_PER_IMAGE)
-            first, last = unit_rows(part)
-            nc.sync.dma_start(
-                out=out[image].rearrange("o h w -> o (h w)")[:, first * W : last * W],
-                in_=result_tiles[slab][:, 0 : last - first, :].rearrange("p i j -> p (i j)"),
-            )
+            top = unit_rows(part)[0]
+            for first, last in pieces(slab):
+                nc.sync.dma_start(
+                    out=out[image].rearrange("o h w -> o (h w)")[:, (top + first) * W : (top + last) * W],
+                    in_=result_tiles[slab][:, first:last, :].rearrange("p i j -> p (i j)"),
+                )
 
         def live(slab):
             return 0 <= slab < N_SLABS

@@ -78,10 +78,10 @@ def tile_gcn_layer_t_e_kernel(tc, x, weight_words, weight_scales, out):
             nc.sync.dma_start(out=raw[:], in_=x[image].rearrange("(p t) h w -> p t (h w)", t=PACK)[:, :, pixels])
             raw_tiles[slab] = raw
 
-        def regroup(copy, slab, first, last):
+        def regroup(copy, slab, first, last, run=4):
             copy(
-                out=grouped_tiles[slab][:, first:last, :].rearrange("p (c i) t -> p c t i", i=4),
-                in_=raw_tiles[slab][:, :, first:last].rearrange("p t (c i) -> p c t i", i=4),
+                out=grouped_tiles[slab][:, first:last, :].rearrange("p (c i) t -> p c t i", i=run),
+                in_=raw_tiles[slab][:, :, first:last].rearrange("p t (c i) -> p c t i", i=run),
             )
 
         def quantise(slab):
@@ -243,11 +243,11 @@ def tile_gcn_layer_t_e_kernel(tc, x, weight_words, weight_scales, out):
             if live(step):
                 grouped_tiles[step] = grouped_pool.tile([P, SLAB_PIXELS, PACK], BF16, align_bytes=64, name="grouped")
                 regroup(nc.vector.tensor_copy, step, 0, VECTOR_PIXELS)
-                regroup(nc.scalar.copy, step, VECTOR_PIXELS, VECTOR_PIXELS + SCALAR_HALF)
+                regroup(nc.scalar.copy, step, VECTOR_PIXELS, VECTOR_PIXELS + SCALAR_HALF, run=8)
             if live(step - 4):
                 weigh_rim_columns(step - 4)
             if live(step):
-                regroup(nc.scalar.copy, step, VECTOR_PIXELS + SCALAR_HALF, SLAB_PIXELS)
+                regroup(nc.scalar.copy, step, VECTOR_PIXELS + SCALAR_HALF, SLAB_PIXELS, run=8)
             if live(step - 3):
                 leave_psum(step - 3)
             if live(step - 5) and has_rim_row(step - 5):

@@ -242,7 +242,7 @@ def tile_gcn_layer_t_e_kernel(tc, x, weight_words, weight_scales, out):
                 multiply(step - 2)
             if live(step):
                 grouped_tiles[step] = grouped_pool.tile([P, SLAB_PIXELS, PACK], BF16, align_bytes=64, name="grouped")
-                regroup(nc.vector.tensor_copy, step, 0, VECTOR_PIXELS)
+                regroup(nc.vector.tensor_copy, step, 0, VECTOR_PIXELS, run=8)
                 regroup(nc.scalar.copy, step, VECTOR_PIXELS, VECTOR_PIXELS + SCALAR_HALF, run=8)
             if live(step - 4):
                 weigh_rim_columns(step - 4)

@@ -136,7 +136,8 @@ def tile_gcn_layer_t_e_kernel(tc, x, weight_words, weight_scales, out):
 
         def pieces(slab):
             if slab == N_SLABS - 1:
-                return [(row, row + BANK_ROWS) for row in range(0, n_rows(slab), BANK_ROWS)]
+                cuts = [0, BANK_ROWS, 2 * BANK_ROWS, 2 * BANK_ROWS + BANK_ROWS // 2, n_rows(slab)]
+                return list(zip(cuts[:-1], cuts[1:]))
             return [(0, n_rows(slab))]
 
         def leave_psum(slab):

import math
from contextlib import ExitStack

import concourse.mybir as mybir

F32 = mybir.dt.float32
BF16 = mybir.dt.bfloat16
I32 = mybir.dt.int32
U32 = mybir.dt.uint32
U8 = mybir.dt.uint8
FP8X4 = mybir.dt.float8_e4m3fn_x4
ADD = mybir.AluOpType.add
COPY = mybir.ActivationFunctionType.Copy

P = 128
PACK = 4
IMAGES, C_IN, H, W, C_OUT = 4, 512, 64, 64, 128
FLOPS = 2 * IMAGES * H * W * C_IN * C_OUT

SLAB_ROWS = 16
SLAB_PIXELS = SLAB_ROWS * W
SLABS_PER_IMAGE = H // SLAB_ROWS
N_SLABS = IMAGES * SLABS_PER_IMAGE
BANK_ROWS = 8
BANK_PIXELS = BANK_ROWS * W
PADDED_ROWS = H + 2
LOADS_AHEAD = 4

VECTOR_PIXELS = 544
SCALAR_HALF = (SLAB_PIXELS - VECTOR_PIXELS) // 2

NINTH = 1.0 / 9.0
RIM = math.sqrt(1.5)

PAIRS = W // 2
HALF_SLOT = PAIRS + 2
SLOT = 2 * HALF_SLOT
ODD_AT = 1
EVEN_AT = ODD_AT + PAIRS
MAX_UNIT_ROWS = 3 * BANK_ROWS
N_SUMS_TILES = 5


def unit_rows(slab_in_image):
    first = 0 if slab_in_image == 0 else slab_in_image * SLAB_ROWS - BANK_ROWS
    last = H if slab_in_image == SLABS_PER_IMAGE - 1 else (slab_in_image + 1) * SLAB_ROWS - BANK_ROWS
    return first, last


def tile_gcn_layer_t_e_kernel(tc, x, weight_words, weight_scales, out):
    nc = tc.nc
    with ExitStack() as ctx:
        keep = ctx.enter_context(tc.tile_pool(name="keep", bufs=1))
        raw_pool = ctx.enter_context(tc.tile_pool(name="raw", bufs=LOADS_AHEAD + 1))
        grouped_pool = ctx.enter_context(tc.tile_pool(name="grouped", bufs=4))
        pair_pool = ctx.enter_context(tc.tile_pool(name="pair", bufs=3))
        result_pool = ctx.enter_context(tc.tile_pool(name="result", bufs=4))
        bank_pool = ctx.enter_context(tc.psum_pool(name="bank", bufs=6))
        rim_pool = ctx.enter_context(tc.psum_pool(name="rim", bufs=2))

        w_codes = keep.tile([P, C_OUT * PACK], U8, align_bytes=64)
        w_scales = keep.tile([P, C_OUT], U8, align_bytes=64)
        x_codes = keep.tile([P, IMAGES, PADDED_ROWS * W], U32, align_bytes=64)
        x_scales = keep.tile([P, IMAGES, PADDED_ROWS * W], U8, align_bytes=64)
        sums_tiles = [keep.tile([P, MAX_UNIT_ROWS + 1, SLOT], F32, name="sums%d" % n) for n in range(N_SUMS_TILES)]

        raw_tiles = {}
        grouped_tiles = {}
        banks_of = {}
        rim_of = {}
        pair_tiles = {}
        result_tiles = {}

        def load(slab):
            image, part = divmod(slab, SLABS_PER_IMAGE)
            raw = raw_pool.tile([P, PACK, SLAB_PIXELS], BF16)
            pixels = slice(part * SLAB_PIXELS, (part + 1) * SLAB_PIXELS)
            nc.sync.dma_start(out=raw[:], in_=x[image].rearrange("(p t) h w -> p t (h w)", t=PACK)[:, :, pixels])
            raw_tiles[slab] = raw

        def regroup(copy, slab, first, last, run=4):
            copy(
                out=grouped_tiles[slab][:, first:last, :].rearrange("p (c i) t -> p c t i", i=run),
                in_=raw_tiles[slab][:, :, first:last].rearrange("p t (c i) -> p c t i", i=run),
            )

        def quantise(slab):
            image, part = divmod(slab, SLABS_PER_IMAGE)
            grouped = grouped_tiles[slab]
            first = (1 + part * SLAB_ROWS) * W
            columns = slice(first, first + SLAB_PIXELS)
            nc.vector.quantize_mx(
                out=x_codes[:, image, columns].bitcast(FP8X4),
                scales=x_scales[:, image, columns],
                in_=grouped[:].rearrange("p w t -> p (w t)"),
            )

        def multiply_window(acc, image, padded_row, n_pixels, start, stop):
            columns = slice(padded_row * W, padded_row * W + n_pixels)
            nc.tensor.matmul_mx(
                out=acc,
                lhsT=w_codes[:].bitcast(FP8X4),
                lhsT_scale=w_scales[:],
                rhs=x_codes[:, image, columns].bitcast(FP8X4),
                rhs_scale=x_scales[:, image, columns],
                start=start,
                stop=stop,
            )

        def multiply(slab):
            image, part = divmod(slab, SLABS_PER_IMAGE)
            first, last = unit_rows(part)
            banks = []
            for row in range(first, last, BANK_ROWS):
                acc = bank_pool.tile([P, BANK_PIXELS], F32)
                for shift in range(3):
                    multiply_window(acc[:], image, row + shift, BANK_PIXELS, shift == 0, shift == 2)
                banks.append(acc)
            banks_of[slab] = banks
            if first == 0 or last == H:
                rim = rim_pool.tile([P, W], F32)
                multiply_window(rim[:], image, 1 if first == 0 else H, W, True, True)
                rim_of[slab] = rim

        def sort_by_parity(dst_rows, src, factor):
            by_parity = src.rearrange("p (i m e) -> p e i m", m=PAIRS, e=2)
            for parity, at in ((1, ODD_AT), (0, EVEN_AT)):
                nc.scalar.activation(out=dst_rows[:, :, at : at + PAIRS], in_=by_parity[:, parity], func=COPY, scale=factor)

        def has_rim_row(slab):
            return slab % SLABS_PER_IMAGE in (0, SLABS_PER_IMAGE - 1)

        def n_rows(slab):
            first, last = unit_rows(slab % SLABS_PER_IMAGE)
            return last - first

        def pieces(slab):
            if slab == N_SLABS - 1:
                cuts = [0, BANK_ROWS, 2 * BANK_ROWS, 2 * BANK_ROWS + BANK_ROWS // 2, n_rows(slab)]
                return list(zip(cuts[:-1], cuts[1:]))
            return [(0, n_rows(slab))]

        def leave_psum(slab):
            sums = sums_tiles[slab % N_SUMS_TILES]
            rows = 0
            for acc in banks_of[slab]:
                sort_by_parity(sums[:, rows : rows + BANK_ROWS, :], acc[:], NINTH)
                rows += BANK_ROWS
            if has_rim_row(slab):
                sort_by_parity(sums[:, rows : rows + 1, :], rim_of[slab][:], NINTH * (RIM - 1.0))

        def weigh_rim_columns(slab):
            ranges = pieces(slab)
            if has_rim_row(slab):
                ranges = ranges[:-1] + [(ranges[-1][0], ranges[-1][1] + 1)]
            for first, last in ranges:
                rim_columns = sums_tiles[slab % N_SUMS_TILES][:, first:last, EVEN_AT - 1 : EVEN_AT + 1]
                nc.scalar.mul(out=rim_columns, in_=rim_columns, mul=RIM)

        def add_rim_row(slab):
            rows = n_rows(slab)
            sums = sums_tiles[slab % N_SUMS_TILES]
            near = slice(0, 2) if slab % SLABS_PER_IMAGE == 0 else slice(rows - 2, rows)
            filled = slice(ODD_AT, EVEN_AT + PAIRS)
            nc.vector.tensor_tensor(
                out=sums[:, near, filled],
                in0=sums[:, near, filled],
                in1=sums[:, rows : rows + 1, filled].to_broadcast([P, 2, W]),
                op=ADD,
            )

        def add_pairs(slab):
            sums = sums_tiles[slab % N_SUMS_TILES]
            pair = pair_pool.tile([P, MAX_UNIT_ROWS, PAIRS], F32)
            for first, last in pieces(slab):
                nc.vector.tensor_tensor(
                    out=pair[:, first:last, :],
                    in0=sums[:, first:last, EVEN_AT : EVEN_AT + PAIRS],
                    in1=sums[:, first:last, ODD_AT : ODD_AT + PAIRS],
                    op=ADD,
                )
            pair_tiles[slab] = pair

        def add_neighbours(slab):
            sums = sums_tiles[slab % N_SUMS_TILES]
            result = result_pool.tile([P, MAX_UNIT_ROWS, W], F32)
            for first, last in pieces(slab):
                neighbours = sums[:, first:last, :].rearrange("p i (e q) -> p i e q", e=2)[:, :, :, 0:PAIRS]
                nc.vector.tensor_tensor(
                    out=result[:, first:last, :].rearrange("p i (m e) -> p i m e", e=2),
                    in0=pair_tiles[slab][:, first:last, :].unsqueeze(3).to_broadcast([P, last - first, PAIRS, 2]),
                    in1=neighbours.rearrange("p i e m -> p i m e"),
                    op=ADD,
                )
            result_tiles[slab] = result

        def scale_rim_row(slab):
            row = 0 if slab % SLABS_PER_IMAGE == 0 else n_rows(slab) - 1
            rim_row = result_tiles[slab][:, row : row + 1, :]
            nc.scalar.mul(out=rim_row, in_=rim_row, mul=RIM)

        def scale_rim_columns(slab):
            for first, last in pieces(slab):
                rim_columns = result_tiles[slab][:, first:last, 0 : W : W - 1]
                nc.scalar.mul(out=rim_columns, in_=rim_columns, mul=RIM)

        def store(slab):
            image, part = divmod(slab, SLABS_PER_IMAGE)
            top = unit_rows(part)[0]
            for first, last in pieces(slab):
                nc.sync.dma_start(
                    out=out[image].rearrange("o h w -> o (h w)")[:, (top + first) * W : (top + last) * W],
                    in_=result_tiles[slab][:, first:last, :].rearrange("p i j -> p (i j)"),
                )

        def live(slab):
            return 0 <= slab < N_SLABS


        nc.vector.memset(w_scales[:].bitcast(I32), 0)
        top_and_bottom = slice(0, PADDED_ROWS, PADDED_ROWS - 1)
        nc.vector.memset(x_codes[:].bitcast(I32).rearrange("p b (r w) -> p b r w", r=PADDED_ROWS)[:, :, top_and_bottom, :], 0)
        nc.vector.memset(x_scales[:].bitcast(I32).rearrange("p b (r w) -> p b r w", r=PADDED_ROWS)[:, :, top_and_bottom, :], 0)
        for sums in sums_tiles:
            nc.vector.memset(sums[:, :, 0 : ODD_AT + 1], 0.0)
            nc.vector.memset(sums[:, :, EVEN_AT + PAIRS - 1 : EVEN_AT + PAIRS + 1], 0.0)

        load(0)
        nc.sync.dma_start(out=w_codes[:].bitcast(I32), in_=weight_words[0].rearrange("p n t -> p (n t)").bitcast(I32))
        for quadrant in range(4):
            nc.sync.dma_start(
                out=w_scales[32 * quadrant : 32 * quadrant + 4, :].bitcast(I32),
                in_=weight_scales[0, 4 * quadrant : 4 * quadrant + 4, :].bitcast(I32),
            )
        for slab in range(1, LOADS_AHEAD):
            load(slab)

        for step in range(N_SLABS + 7):
            if live(step + LOADS_AHEAD):
                load(step + LOADS_AHEAD)
            if live(step - 2):
                quantise(step - 2)
                multiply(step - 2)
            if live(step):
                grouped_tiles[step] = grouped_pool.tile([P, SLAB_PIXELS, PACK], BF16, align_bytes=64, name="grouped")
                regroup(nc.vector.tensor_copy, step, 0, VECTOR_PIXELS, run=8)
                regroup(nc.scalar.copy, step, VECTOR_PIXELS, VECTOR_PIXELS + SCALAR_HALF, run=8)
            if live(step - 4):
                weigh_rim_columns(step - 4)
            if live(step):
                regroup(nc.scalar.copy, step, VECTOR_PIXELS + SCALAR_HALF, SLAB_PIXELS, run=8)
            if live(step - 3):
                leave_psum(step - 3)
            if live(step - 5) and has_rim_row(step - 5):
                add_rim_row(step - 5)
            if live(step - 6):
                add_neighbours(step - 6)
            if live(step - 5):
                add_pairs(step - 5)
            if live(step - 6):
                if has_rim_row(step - 6):
                    scale_rim_row(step - 6)
                scale_rim_columns(step - 6)
                store(step - 6)
